import numpy as np
import ml_dtypes


def mxq(x, axis, fmt="e4m3"):
    dtype, down = {"e4m3": (ml_dtypes.float8_e4m3fn, 7), "e5m2": (ml_dtypes.float8_e5m2, 14)}[fmt]
    v = np.moveaxis(np.asarray(x, np.float32).astype(ml_dtypes.bfloat16).astype(np.float64), axis, -1)
    blocks = v.reshape(v.shape[:-1] + (-1, 32))
    amax = np.abs(blocks).max(-1, keepdims=True)
    byte = np.maximum(np.where(amax > 0, np.frexp(amax)[1] - 1 + 127, 0) - down, 1)
    scale = np.exp2(byte - 127.0)
    codes = (blocks / scale).astype(np.float32).astype(dtype).astype(np.float64)
    return np.moveaxis((codes * scale).reshape(v.shape), -1, axis)


WIDE = False


def mx_kscale(k):
    if not WIDE:
        return np.ones(k)
    levels = np.array([10, -10, 5, -5, 0])
    a = np.random.permutation(np.resize(levels, k // 512 * 4)).reshape(k // 512, 4)
    idx = np.arange(k)
    return np.exp2(a[idx // 512, idx % 128 // 32])


BF16 = ml_dtypes.bfloat16


def bf(x):
    return np.asarray(x, np.float32).astype(BF16)


def f64(x):
    return np.asarray(x).astype(np.float64)


N, MI, MO, LMAX = 1024, 512, 128, 3
C = (LMAX + 1) ** 2


def setup_inputs():
    s = mx_kscale(MI)
    d = {"x": bf(np.random.standard_normal((N, MI, C)) * s[None, :, None])}
    for l in range(LMAX + 1):
        d["w%d" % l] = bf(np.random.standard_normal((MI, MO)) / np.sqrt(MI) / s[:, None])
    return d


def reference(x, w0, w1, w2, w3):
    xq = mxq(f64(x), 1, "e4m3")
    parts = []
    for l, w in enumerate([w0, w1, w2, w3]):
        xl = xq[:, :, l * l:(l + 1) ** 2].transpose(0, 2, 1)
        parts.append((xl @ mxq(f64(w), 0, "e4m3")).transpose(0, 2, 1))
    return np.concatenate(parts, axis=2)

@@ -1,0 +1,144 @@
+from contextlib import ExitStack
+
+import concourse.bass as bass
+import concourse.mybir as mybir
+import concourse.tile as tile
+from concourse.masks import make_identity
+
+F32 = mybir.dt.float32
+BF16 = mybir.dt.bfloat16
+U32 = mybir.dt.uint32
+U8 = mybir.dt.uint8
+FP8X4 = mybir.dt.float8_e4m3fn_x4
+
+P = 128
+N, MI, MO, C = 1024, 512, 128, 16
+PACK = 4
+NT = N // P
+HALF_C = 8
+UNITS = NT * 2
+DEGREE = [0, 1, 1, 1, 2, 2, 2, 2, 2, 3, 3, 3, 3, 3, 3, 3]
+
+FLOPS = 2 * N * C * MI * MO
+
+
+def tile_irrepsstridelinear_kernel(tc, x, w0, w1, w2, w3, out):
+    nc = tc.nc
+    with ExitStack() as ctx:
+        ctx.enter_context(tc.manual_schedule())
+        const = ctx.enter_context(tc.tile_pool(name="const", bufs=1))
+        xpool = ctx.enter_context(tc.tile_pool(name="xpool", bufs=1))
+        gpool = ctx.enter_context(tc.tile_pool(name="gpool", bufs=3))
+        qpool = ctx.enter_context(tc.tile_pool(name="qpool", bufs=3))
+        opool = ctx.enter_context(tc.tile_pool(name="opool", bufs=3))
+        tps = ctx.enter_context(tc.psum_pool(name="tps", bufs=4))
+        ops = ctx.enter_context(tc.psum_pool(name="ops", bufs=4))
+
+        xs = []
+        for m in range(NT):
+            xt = xpool.tile([P, MI * C], BF16, name="x%d" % m)
+            nc.sync.dma_start(out=xt[:], in_=x[m * P:(m + 1) * P].rearrange("n i c -> n (i c)"))
+            xs.append(xt)
+        wraw = const.tile([P, 4, PACK, MO], BF16, name="wraw")
+        for l, w in enumerate([w0, w1, w2, w3]):
+            nc.scalar.dma_start(out=wraw[:, l], in_=w.rearrange("(p j) o -> p j o", j=PACK))
+
+        ident = const.tile([P, P], F32, name="ident")
+        make_identity(nc, ident[:])
+
+        wgrp = const.tile([P, 4, MO, PACK], BF16, name="wgrp", align_bytes=64)
+        nc.vector.tensor_copy(out=wgrp[:], in_=wraw[:].rearrange("p l j o -> p l o j"))
+        wcodes = const.tile([P, 4 * MO], U32, name="wcodes", align_bytes=64)
+        wscales = const.tile([P, 4 * MO], U8, name="wscales", align_bytes=64)
+        nc.vector.quantize_mx(
+            out=wcodes[:].bitcast(FP8X4),
+            scales=wscales[:],
+            in_=wgrp[:].rearrange("p l o j -> p (l o j)"),
+        )
+
+        banks = {}
+        grouped = {}
+        quant = {}
+        accs = {}
+        staged = {}
+
+        def transposes(u):
+            m, h = divmod(u, 2)
+            words = xs[m][:].bitcast(F32)
+            for b in range(4):
+                cp = 4 * h + b
+                bank = tps.tile([P, PACK * P], F32, name="bank", tag="bank")
+                for t in range(PACK):
+                    first = 8 * t + cp
+                    nc.tensor.transpose(
+                        bank[:, t * P:(t + 1) * P],
+                        words[:, first:first + 32 * (P - 1) + 1:32],
+                        ident[:],
+                    )
+                banks[(u, b)] = bank
+
+        def regroup(u):
+            g = gpool.tile([P, HALF_C * P * PACK], BF16, name="g", tag="g", align_bytes=64)
+            grouped[u] = g
+            for b in range(4):
+                src = banks.pop((u, b))[:].bitcast(BF16).rearrange(
+                    "p (t n e) -> p e n t", t=PACK, n=P, e=2)
+                dst = g[:, b * 1024:(b + 1) * 1024].rearrange(
+                    "p (e n t) -> p e n t", e=2, n=P, t=PACK)
+                if b % 2 == 0:
+                    nc.vector.tensor_copy(out=dst, in_=src)
+                else:
+                    nc.scalar.copy(out=dst, in_=src)
+
+        def quantise(u):
+            codes = qpool.tile([P, HALF_C * P], U32, name="codes", tag="codes", align_bytes=64)
+            scales = qpool.tile([P, HALF_C * P], U8, name="scales", tag="scales", align_bytes=64)
+            nc.vector.quantize_mx(out=codes[:].bitcast(FP8X4), scales=scales[:], in_=grouped.pop(u)[:])
+            quant[u] = (codes, scales)
+
+        def multiply(u):
+            h = u % 2
+            codes, scales = quant.pop(u)
+            for b in range(2):
+                acc = ops.tile([P, 4 * MO], F32, name="acc", tag="acc")
+                for cc in range(4):
+                    cl = 4 * b + cc
+                    l = DEGREE[HALF_C * h + cl]
+                    nc.tensor.matmul_mx(
+                        out=acc[:, cc * MO:(cc + 1) * MO],
+                        lhsT=codes[:, cl * P:(cl + 1) * P].bitcast(FP8X4),
+                        lhsT_scale=scales[:, cl * P:(cl + 1) * P],
+                        rhs=wcodes[:, l * MO:(l + 1) * MO].bitcast(FP8X4),
+                        rhs_scale=wscales[:, l * MO:(l + 1) * MO],
+                        start=True,
+                        stop=True,
+                    )
+                accs[(u, b)] = acc
+
+        def drain(u):
+            m, h = divmod(u, 2)
+            if h == 0:
+                staged[m] = opool.tile([P, MO * C], F32, name="osb", tag="osb")
+            osb = staged[m]
+            view = osb[:].rearrange("p (o c) -> p o c", c=C)
+            for b in range(2):
+                c0 = HALF_C * h + 4 * b
+                nc.scalar.copy(
+                    out=view[:, :, c0:c0 + 4],
+                    in_=accs.pop((u, b))[:].rearrange("p (cc o) -> p o cc", cc=4),
+                )
+            if h == 1:
+                nc.scalar.dma_start(
+                    out=out[m * P:(m + 1) * P].rearrange("n o c -> n (o c)"), in_=osb[:])
+
+        transposes(0)
+        for k in range(UNITS + 2):
+            if k < UNITS:
+                regroup(k)
+            if k + 1 < UNITS:
+                transposes(k + 1)
+            if 0 <= k - 1 < UNITS:
+                quantise(k - 1)
+                multiply(k - 1)
+            if 0 <= k - 2 < UNITS:
+                drain(k - 2)

@@ -1,8 +1,6 @@
 from contextlib import ExitStack
 
-import concourse.bass as bass
 import concourse.mybir as mybir
-import concourse.tile as tile
 from concourse.masks import make_identity
 
 F32 = mybir.dt.float32
@@ -10,16 +8,18 @@ BF16 = mybir.dt.bfloat16
 U32 = mybir.dt.uint32
 U8 = mybir.dt.uint8
 FP8X4 = mybir.dt.float8_e4m3fn_x4
+ALU = mybir.AluOpType
 
 P = 128
 N, MI, MO, C = 1024, 512, 128, 16
 PACK = 4
 NT = N // P
-HALF_C = 8
-UNITS = NT * 2
 DEGREE = [0, 1, 1, 1, 2, 2, 2, 2, 2, 3, 3, 3, 3, 3, 3, 3]
+BANK = 2 * P * PACK
 
 FLOPS = 2 * N * C * MI * MO
+
+UNITS = [(m, 4 * h, 4) for m in range(NT - 1) for h in range(2)] + [(NT - 1, 2 * q, 2) for q in range(4)]
 
 
 def tile_irrepsstridelinear_kernel(tc, x, w0, w1, w2, w3, out):
@@ -30,31 +30,36 @@ def tile_irrepsstridelinear_kernel(tc, x, w0, w1, w2, w3, out):
         xpool = ctx.enter_context(tc.tile_pool(name="xpool", bufs=1))
         gpool = ctx.enter_context(tc.tile_pool(name="gpool", bufs=3))
         qpool = ctx.enter_context(tc.tile_pool(name="qpool", bufs=3))
-        opool = ctx.enter_context(tc.tile_pool(name="opool", bufs=3))
+        opool = ctx.enter_context(tc.tile_pool(name="opool", bufs=5))
         tps = ctx.enter_context(tc.psum_pool(name="tps", bufs=4))
         ops = ctx.enter_context(tc.psum_pool(name="ops", bufs=4))
 
         xs = []
+        wraw = const.tile([P, 4, PACK, MO], BF16, name="wraw")
         for m in range(NT):
             xt = xpool.tile([P, MI * C], BF16, name="x%d" % m)
             nc.sync.dma_start(out=xt[:], in_=x[m * P:(m + 1) * P].rearrange("n i c -> n (i c)"))
             xs.append(xt)
-        wraw = const.tile([P, 4, PACK, MO], BF16, name="wraw")
-        for l, w in enumerate([w0, w1, w2, w3]):
-            nc.scalar.dma_start(out=wraw[:, l], in_=w.rearrange("(p j) o -> p j o", j=PACK))
+            if m == 0:
+                for l, w in enumerate([w0, w1, w2, w3]):
+                    nc.sync.dma_start(out=wraw[:, l], in_=w.rearrange("(p j) o -> p j o", j=PACK))
 
         ident = const.tile([P, P], F32, name="ident")
         make_identity(nc, ident[:])
 
         wgrp = const.tile([P, 4, MO, PACK], BF16, name="wgrp", align_bytes=64)
-        nc.vector.tensor_copy(out=wgrp[:], in_=wraw[:].rearrange("p l j o -> p l o j"))
         wcodes = const.tile([P, 4 * MO], U32, name="wcodes", align_bytes=64)
         wscales = const.tile([P, 4 * MO], U8, name="wscales", align_bytes=64)
-        nc.vector.quantize_mx(
-            out=wcodes[:].bitcast(FP8X4),
-            scales=wscales[:],
-            in_=wgrp[:].rearrange("p l o j -> p (l o j)"),
-        )
+        nc.gpsimd.tensor_scalar(
+            out=wgrp[:], in0=wraw[:].rearrange("p l j o -> p l o j"),
+            scalar1=1.0, scalar2=0.0, op0=ALU.mult, op1=ALU.add)
+
+        def quantise_weights():
+            nc.vector.quantize_mx(
+                out=wcodes[:].bitcast(FP8X4),
+                scales=wscales[:],
+                in_=wgrp[:].rearrange("p l o j -> p (l o j)"),
+            )
 
         banks = {}
         grouped = {}
@@ -63,27 +68,29 @@ def tile_irrepsstridelinear_kernel(tc, x, w0, w1, w2, w3, out):
         staged = {}
 
         def transposes(u):
-            m, h = divmod(u, 2)
+            m, cp0, nb = UNITS[u]
             words = xs[m][:].bitcast(F32)
-            for b in range(4):
-                cp = 4 * h + b
+            for b in range(nb):
+                cp = cp0 + b
                 bank = tps.tile([P, PACK * P], F32, name="bank", tag="bank")
                 for t in range(PACK):
                     first = 8 * t + cp
+                    step = 32
                     nc.tensor.transpose(
                         bank[:, t * P:(t + 1) * P],
-                        words[:, first:first + 32 * (P - 1) + 1:32],
+                        words[:, first:first + step * (P - 1) + 1:step],
                         ident[:],
                     )
                 banks[(u, b)] = bank
 
         def regroup(u):
-            g = gpool.tile([P, HALF_C * P * PACK], BF16, name="g", tag="g", align_bytes=64)
+            m, cp0, nb = UNITS[u]
+            g = gpool.tile([P, 4 * BANK], BF16, name="g", tag="g", align_bytes=64)
             grouped[u] = g
-            for b in range(4):
-                src = banks.pop((u, b))[:].bitcast(BF16).rearrange(
+            for b in range(nb):
+                src = banks[(u, b)][:].bitcast(BF16).rearrange(
                     "p (t n e) -> p e n t", t=PACK, n=P, e=2)
-                dst = g[:, b * 1024:(b + 1) * 1024].rearrange(
+                dst = g[:, b * BANK:(b + 1) * BANK].rearrange(
                     "p (e n t) -> p e n t", e=2, n=P, t=PACK)
                 if b % 2 == 0:
                     nc.vector.tensor_copy(out=dst, in_=src)
@@ -91,19 +98,23 @@ def tile_irrepsstridelinear_kernel(tc, x, w0, w1, w2, w3, out):
                     nc.scalar.copy(out=dst, in_=src)
 
         def quantise(u):
-            codes = qpool.tile([P, HALF_C * P], U32, name="codes", tag="codes", align_bytes=64)
-            scales = qpool.tile([P, HALF_C * P], U8, name="scales", tag="scales", align_bytes=64)
-            nc.vector.quantize_mx(out=codes[:].bitcast(FP8X4), scales=scales[:], in_=grouped.pop(u)[:])
+            m, cp0, nb = UNITS[u]
+            codes = qpool.tile([P, BANK], U32, name="codes", tag="codes", align_bytes=64)
+            scales = qpool.tile([P, BANK], U8, name="scales", tag="scales", align_bytes=64)
+            wide = nb * BANK // PACK
+            nc.vector.quantize_mx(
+                out=codes[:, :wide].bitcast(FP8X4), scales=scales[:, :wide],
+                in_=grouped[u][:, :nb * BANK])
             quant[u] = (codes, scales)
 
         def multiply(u):
-            h = u % 2
-            codes, scales = quant.pop(u)
-            for b in range(2):
+            m, cp0, nb = UNITS[u]
+            codes, scales = quant[u]
+            for b in range(nb // 2):
                 acc = ops.tile([P, 4 * MO], F32, name="acc", tag="acc")
                 for cc in range(4):
                     cl = 4 * b + cc
-                    l = DEGREE[HALF_C * h + cl]
+                    l = DEGREE[2 * cp0 + cl]
                     nc.tensor.matmul_mx(
                         out=acc[:, cc * MO:(cc + 1) * MO],
                         lhsT=codes[:, cl * P:(cl + 1) * P].bitcast(FP8X4),
@@ -116,29 +127,32 @@ def tile_irrepsstridelinear_kernel(tc, x, w0, w1, w2, w3, out):
                 accs[(u, b)] = acc
 
         def drain(u):
-            m, h = divmod(u, 2)
-            if h == 0:
+            m, cp0, nb = UNITS[u]
+            if cp0 == 0:
                 staged[m] = opool.tile([P, MO * C], F32, name="osb", tag="osb")
             osb = staged[m]
             view = osb[:].rearrange("p (o c) -> p o c", c=C)
-            for b in range(2):
-                c0 = HALF_C * h + 4 * b
+            for b in range(nb // 2):
+                c0 = 2 * cp0 + 4 * b
                 nc.scalar.copy(
                     out=view[:, :, c0:c0 + 4],
-                    in_=accs.pop((u, b))[:].rearrange("p (cc o) -> p o cc", cc=4),
+                    in_=accs[(u, b)][:].rearrange("p (cc o) -> p o cc", cc=4),
                 )
-            if h == 1:
-                nc.scalar.dma_start(
+            if cp0 + nb == C // 2:
+                nc.sync.dma_start(
                     out=out[m * P:(m + 1) * P].rearrange("n o c -> n (o c)"), in_=osb[:])
 
+        count = len(UNITS)
         transposes(0)
-        for k in range(UNITS + 2):
-            if k < UNITS:
+        for k in range(count + 2):
+            if k < count:
                 regroup(k)
-            if k + 1 < UNITS:
+            if k + 1 < count:
                 transposes(k + 1)
-            if 0 <= k - 1 < UNITS:
+            if k == 1:
+                quantise_weights()
+            if 0 <= k - 1 < count:
                 quantise(k - 1)
                 multiply(k - 1)
-            if 0 <= k - 2 < UNITS:
+            if 0 <= k - 2 < count:
                 drain(k - 2)

@@ -42,7 +42,7 @@ def tile_irrepsstridelinear_kernel(tc, x, w0, w1, w2, w3, out):
             xs.append(xt)
             if m == 0:
                 for l, w in enumerate([w0, w1, w2, w3]):
-                    nc.sync.dma_start(out=wraw[:, l], in_=w.rearrange("(p j) o -> p j o", j=PACK))
+                    nc.sync.dma_start(out=wraw[:, l], in_=w.rearrange("(j p) o -> p j o", j=PACK))
 
         ident = const.tile([P, P], F32, name="ident")
         make_identity(nc, ident[:])
@@ -74,8 +74,8 @@ def tile_irrepsstridelinear_kernel(tc, x, w0, w1, w2, w3, out):
                 cp = cp0 + b
                 bank = tps.tile([P, PACK * P], F32, name="bank", tag="bank")
                 for t in range(PACK):
-                    first = 8 * t + cp
-                    step = 32
+                    first = 8 * P * t + cp
+                    step = 8
                     nc.tensor.transpose(
                         bank[:, t * P:(t + 1) * P],
                         words[:, first:first + step * (P - 1) + 1:step],

@@ -19,7 +19,7 @@ BANK = 2 * P * PACK
 
 FLOPS = 2 * N * C * MI * MO
 
-UNITS = [(m, 4 * h, 4) for m in range(NT - 1) for h in range(2)] + [(NT - 1, 2 * q, 2) for q in range(4)]
+UNITS = [(m, 4 * h, 4) for m in range(NT - 1) for h in range(2)] + [(NT - 1, 0, 4), (NT - 1, 4, 2), (NT - 1, 6, 2)]
 
 
 def tile_irrepsstridelinear_kernel(tc, x, w0, w1, w2, w3, out):
@@ -38,7 +38,11 @@ def tile_irrepsstridelinear_kernel(tc, x, w0, w1, w2, w3, out):
         wraw = const.tile([P, 4, PACK, MO], BF16, name="wraw")
         for m in range(NT):
             xt = xpool.tile([P, MI * C], BF16, name="x%d" % m)
-            nc.sync.dma_start(out=xt[:], in_=x[m * P:(m + 1) * P].rearrange("n i c -> n (i c)"))
+            rows = x[m * P:(m + 1) * P].rearrange("n i c -> n (i c)")
+            pieces = PACK if m == 0 else 1
+            wide = MI * C // pieces
+            for t in range(pieces):
+                nc.sync.dma_start(out=xt[:, t * wide:(t + 1) * wide], in_=rows[:, t * wide:(t + 1) * wide])
             xs.append(xt)
             if m == 0:
                 for l, w in enumerate([w0, w1, w2, w3]):
@@ -71,17 +75,17 @@ def tile_irrepsstridelinear_kernel(tc, x, w0, w1, w2, w3, out):
             m, cp0, nb = UNITS[u]
             words = xs[m][:].bitcast(F32)
             for b in range(nb):
-                cp = cp0 + b
-                bank = tps.tile([P, PACK * P], F32, name="bank", tag="bank")
-                for t in range(PACK):
-                    first = 8 * P * t + cp
-                    step = 8
-                    nc.tensor.transpose(
-                        bank[:, t * P:(t + 1) * P],
-                        words[:, first:first + step * (P - 1) + 1:step],
-                        ident[:],
-                    )
-                banks[(u, b)] = bank
+                banks[(u, b)] = tps.tile([P, PACK * P], F32, name="bank", tag="bank")
+            order = [(b, t) for b in range(nb) for t in range(PACK)]
+            if u == 0:
+                order = [(b, t) for t in range(PACK) for b in range(nb)]
+            for b, t in order:
+                first = 8 * P * t + cp0 + b
+                nc.tensor.transpose(
+                    banks[(u, b)][:, t * P:(t + 1) * P],
+                    words[:, first:first + 8 * (P - 1) + 1:8],
+                    ident[:],
+                )
 
         def regroup(u):
             m, cp0, nb = UNITS[u]

@@ -31,8 +31,8 @@ def tile_irrepsstridelinear_kernel(tc, x, w0, w1, w2, w3, out):
         gpool = ctx.enter_context(tc.tile_pool(name="gpool", bufs=3))
         qpool = ctx.enter_context(tc.tile_pool(name="qpool", bufs=3))
         opool = ctx.enter_context(tc.tile_pool(name="opool", bufs=5))
-        tps = ctx.enter_context(tc.psum_pool(name="tps", bufs=4))
-        ops = ctx.enter_context(tc.psum_pool(name="ops", bufs=4))
+        tps = ctx.enter_context(tc.psum_pool(name="tps", bufs=6))
+        ops = ctx.enter_context(tc.psum_pool(name="ops", bufs=2))
 
         xs = []
         wraw = const.tile([P, 4, PACK, MO], BF16, name="wraw")

@@ -29,10 +29,10 @@ def tile_irrepsstridelinear_kernel(tc, x, w0, w1, w2, w3, out):
         const = ctx.enter_context(tc.tile_pool(name="const", bufs=1))
         xpool = ctx.enter_context(tc.tile_pool(name="xpool", bufs=1))
         gpool = ctx.enter_context(tc.tile_pool(name="gpool", bufs=3))
-        qpool = ctx.enter_context(tc.tile_pool(name="qpool", bufs=3))
+        qpool = ctx.enter_context(tc.tile_pool(name="qpool", bufs=4))
         opool = ctx.enter_context(tc.tile_pool(name="opool", bufs=5))
-        tps = ctx.enter_context(tc.psum_pool(name="tps", bufs=6))
-        ops = ctx.enter_context(tc.psum_pool(name="ops", bufs=2))
+        tps = ctx.enter_context(tc.psum_pool(name="tps", bufs=4))
+        ops = ctx.enter_context(tc.psum_pool(name="ops", bufs=4))
 
         xs = []
         wraw = const.tile([P, 4, PACK, MO], BF16, name="wraw")
@@ -147,8 +147,12 @@ def tile_irrepsstridelinear_kernel(tc, x, w0, w1, w2, w3, out):
                     out=out[m * P:(m + 1) * P].rearrange("n o c -> n (o c)"), in_=osb[:])
 
         count = len(UNITS)
+        held = []
+        pending = []
         transposes(0)
-        for k in range(count + 2):
+        for k in range(count + 3):
+            ready = pending[:1]
+            pending = pending[1:]
             if k < count:
                 regroup(k)
             if k + 1 < count:
@@ -157,6 +161,12 @@ def tile_irrepsstridelinear_kernel(tc, x, w0, w1, w2, w3, out):
                 quantise_weights()
             if 0 <= k - 1 < count:
                 quantise(k - 1)
-                multiply(k - 1)
-            if 0 <= k - 2 < count:
-                drain(k - 2)
+                held.append(k - 1)
+                m, cp0, nb = UNITS[k - 1]
+                if m == NT - 1 or cp0 > 0:
+                    for u in held:
+                        multiply(u)
+                        pending.append(u)
+                    held = []
+            for u in ready:
+                drain(u)

from contextlib import ExitStack

import concourse.mybir as mybir
from concourse.masks import make_identity

F32 = mybir.dt.float32
BF16 = mybir.dt.bfloat16
U32 = mybir.dt.uint32
U8 = mybir.dt.uint8
FP8X4 = mybir.dt.float8_e4m3fn_x4
ALU = mybir.AluOpType

P = 128
N, MI, MO, C = 1024, 512, 128, 16
PACK = 4
NT = N // P
DEGREE = [0, 1, 1, 1, 2, 2, 2, 2, 2, 3, 3, 3, 3, 3, 3, 3]
BANK = 2 * P * PACK

FLOPS = 2 * N * C * MI * MO

UNITS = [(m, 4 * h, 4) for m in range(NT - 1) for h in range(2)] + [(NT - 1, 0, 4), (NT - 1, 4, 2), (NT - 1, 6, 2)]


def tile_irrepsstridelinear_kernel(tc, x, w0, w1, w2, w3, out):
    nc = tc.nc
    with ExitStack() as ctx:
        ctx.enter_context(tc.manual_schedule())
        const = ctx.enter_context(tc.tile_pool(name="const", bufs=1))
        xpool = ctx.enter_context(tc.tile_pool(name="xpool", bufs=1))
        gpool = ctx.enter_context(tc.tile_pool(name="gpool", bufs=3))
        qpool = ctx.enter_context(tc.tile_pool(name="qpool", bufs=4))
        opool = ctx.enter_context(tc.tile_pool(name="opool", bufs=5))
        tps = ctx.enter_context(tc.psum_pool(name="tps", bufs=4))
        ops = ctx.enter_context(tc.psum_pool(name="ops", bufs=4))

        xs = []
        wraw = const.tile([P, 4, PACK, MO], BF16, name="wraw")
        for m in range(NT):
            xt = xpool.tile([P, MI * C], BF16, name="x%d" % m)
            rows = x[m * P:(m + 1) * P].rearrange("n i c -> n (i c)")
            pieces = PACK if m == 0 else 1
            wide = MI * C // pieces
            for t in range(pieces):
                nc.sync.dma_start(out=xt[:, t * wide:(t + 1) * wide], in_=rows[:, t * wide:(t + 1) * wide])
            xs.append(xt)
            if m == 0:
                for l, w in enumerate([w0, w1, w2, w3]):
                    nc.sync.dma_start(out=wraw[:, l], in_=w.rearrange("(j p) o -> p j o", j=PACK))

        ident = const.tile([P, P], F32, name="ident")
        make_identity(nc, ident[:])

        wgrp = const.tile([P, 4, MO, PACK], BF16, name="wgrp", align_bytes=64)
        wcodes = const.tile([P, 4 * MO], U32, name="wcodes", align_bytes=64)
        wscales = const.tile([P, 4 * MO], U8, name="wscales", align_bytes=64)
        nc.gpsimd.tensor_scalar(
            out=wgrp[:], in0=wraw[:].rearrange("p l j o -> p l o j"),
            scalar1=1.0, scalar2=0.0, op0=ALU.mult, op1=ALU.add)

        def quantise_weights():
            nc.vector.quantize_mx(
                out=wcodes[:].bitcast(FP8X4),
                scales=wscales[:],
                in_=wgrp[:].rearrange("p l o j -> p (l o j)"),
            )

        banks = {}
        grouped = {}
        quant = {}
        accs = {}
        staged = {}

        def transposes(u):
            m, cp0, nb = UNITS[u]
            words = xs[m][:].bitcast(F32)
            for b in range(nb):
                banks[(u, b)] = tps.tile([P, PACK * P], F32, name="bank", tag="bank")
            order = [(b, t) for b in range(nb) for t in range(PACK)]
            if u == 0:
                order = [(b, t) for t in range(PACK) for b in range(nb)]
            for b, t in order:
                first = 8 * P * t + cp0 + b
                nc.tensor.transpose(
                    banks[(u, b)][:, t * P:(t + 1) * P],
                    words[:, first:first + 8 * (P - 1) + 1:8],
                    ident[:],
                )

        def regroup(u):
            m, cp0, nb = UNITS[u]
            g = gpool.tile([P, 4 * BANK], BF16, name="g", tag="g", align_bytes=64)
            grouped[u] = g
            for b in range(nb):
                src = banks[(u, b)][:].bitcast(BF16).rearrange(
                    "p (t n e) -> p e n t", t=PACK, n=P, e=2)
                dst = g[:, b * BANK:(b + 1) * BANK].rearrange(
                    "p (e n t) -> p e n t", e=2, n=P, t=PACK)
                if b % 2 == 0:
                    nc.vector.tensor_copy(out=dst, in_=src)
                else:
                    nc.scalar.copy(out=dst, in_=src)

        def quantise(u):
            m, cp0, nb = UNITS[u]
            codes = qpool.tile([P, BANK], U32, name="codes", tag="codes", align_bytes=64)
            scales = qpool.tile([P, BANK], U8, name="scales", tag="scales", align_bytes=64)
            wide = nb * BANK // PACK
            nc.vector.quantize_mx(
                out=codes[:, :wide].bitcast(FP8X4), scales=scales[:, :wide],
                in_=grouped[u][:, :nb * BANK])
            quant[u] = (codes, scales)

        def multiply(u):
            m, cp0, nb = UNITS[u]
            codes, scales = quant[u]
            for b in range(nb // 2):
                acc = ops.tile([P, 4 * MO], F32, name="acc", tag="acc")
                for cc in range(4):
                    cl = 4 * b + cc
                    l = DEGREE[2 * cp0 + cl]
                    nc.tensor.matmul_mx(
                        out=acc[:, cc * MO:(cc + 1) * MO],
                        lhsT=codes[:, cl * P:(cl + 1) * P].bitcast(FP8X4),
                        lhsT_scale=scales[:, cl * P:(cl + 1) * P],
                        rhs=wcodes[:, l * MO:(l + 1) * MO].bitcast(FP8X4),
                        rhs_scale=wscales[:, l * MO:(l + 1) * MO],
                        start=True,
                        stop=True,
                    )
                accs[(u, b)] = acc

        def drain(u):
            m, cp0, nb = UNITS[u]
            if cp0 == 0:
                staged[m] = opool.tile([P, MO * C], F32, name="osb", tag="osb")
            osb = staged[m]
            view = osb[:].rearrange("p (o c) -> p o c", c=C)
            for b in range(nb // 2):
                c0 = 2 * cp0 + 4 * b
                nc.scalar.copy(
                    out=view[:, :, c0:c0 + 4],
                    in_=accs[(u, b)][:].rearrange("p (cc o) -> p o cc", cc=4),
                )
            if cp0 + nb == C // 2:
                nc.sync.dma_start(
                    out=out[m * P:(m + 1) * P].rearrange("n o c -> n (o c)"), in_=osb[:])

        count = len(UNITS)
        held = []
        pending = []
        transposes(0)
        for k in range(count + 3):
            ready = pending[:1]
            pending = pending[1:]
            if k < count:
                regroup(k)
            if k + 1 < count:
                transposes(k + 1)
            if k == 1:
                quantise_weights()
            if 0 <= k - 1 < count:
                quantise(k - 1)
                held.append(k - 1)
                m, cp0, nb = UNITS[k - 1]
                if m == NT - 1 or cp0 > 0:
                    for u in held:
                        multiply(u)
                        pending.append(u)
                    held = []
            for u in ready:
                drain(u)
